import numpy as np
import ml_dtypes

BF16 = ml_dtypes.bfloat16


def bf(x):
    return np.asarray(x, np.float32).astype(BF16)


def f32(x):
    return np.asarray(x, np.float32)


def f64(x):
    return np.asarray(x).astype(np.float64)


def striped(idx):
    return np.tile(idx.reshape(-1, 16).T, (8, 1))


C, S, N = 256, 512, 256


def setup_inputs():
    return {
        "embed": f32(np.random.standard_normal((C, S))),
        "gain": f32(1.0 + 0.1 * np.random.standard_normal((C, 1))),
        "w_head": bf(np.random.standard_normal((C, S)) / np.sqrt(C)),
        "b_head": f32(0.1 * np.random.standard_normal((S, 1))),
        "offs": striped(np.random.permutation(np.tile(np.arange(S), 2))[:N]),
    }


def reference(embed, gain, w_head, b_head, offs):
    idx = offs[:16].T.reshape(-1)
    h = f64(embed)[:, idx]
    t = h * f64(gain)
    r = 1.0 / np.sqrt(np.mean(h * h, axis=0, keepdims=True))
    return f64(w_head).T @ (t * r) + f64(b_head)

@@ -1,0 +1,76 @@
+import math
+
+import concourse.mybir as mybir
+
+P = 128
+C, S, N = 256, 512, 256
+KB = C // P
+MB = S // P
+FLOPS = 2 * C * S * N
+
+F32, BF16, U16 = mybir.dt.float32, mybir.dt.bfloat16, mybir.dt.uint16
+MULT = mybir.AluOpType.mult
+ACT = mybir.ActivationFunctionType
+
+
+def tile_llama_mla_kernel(tc, embed, gain, w_head, b_head, offs, out):
+    nc = tc.nc
+    with (
+        tc.tile_pool(name="held", bufs=1) as held,
+        tc.psum_pool(name="psum", bufs=1) as psum,
+    ):
+        offsets = held.tile([P, N // 16], U16, name="offsets")
+        nc.sync.dma_start(offsets[:], offs)
+        gain_sb = held.tile([P, KB], F32, name="gain_sb")
+        nc.scalar.dma_start(gain_sb[:], gain.rearrange("(p k) o -> p (k o)", k=KB))
+
+        embed_blocks = embed.rearrange("(p k) s -> k p s", k=KB)
+        table = [held.tile([P, S], F32, name=f"table{k}") for k in range(KB)]
+        nc.sync.dma_start(table[0][:], embed_blocks[0])
+        nc.scalar.dma_start(table[1][:], embed_blocks[1])
+
+        w_sb = held.tile([P, KB, S], BF16, name="w_sb")
+        nc.sync.dma_start(w_sb[:], w_head.rearrange("(p k) v -> p k v", k=KB))
+        bias_sb = held.tile([P, MB], F32, name="bias_sb")
+        with nc.allow_non_contiguous_dma(reason="512 bias values, one to a partition"):
+            nc.scalar.dma_start(bias_sb[:], b_head.rearrange("(m p) o -> p (m o)", p=P))
+
+        ones = held.tile([P, P], BF16, name="ones")
+        nc.vector.memset(ones[:], 1.0)
+        root_mean = held.tile([P, N], F32, name="root_mean")
+        nc.vector.memset(root_mean[:], 1.0 / math.sqrt(C))
+        gain_cols = [held.tile([P, N], F32, name=f"gain_cols{k}") for k in range(KB)]
+        for k in range(KB):
+            nc.gpsimd.tensor_copy(gain_cols[k][:], gain_sb[:, k : k + 1].to_broadcast([P, N]))
+
+        mean_ps = psum.tile([P, N], F32, name="mean_ps")
+        for k in range(KB):
+            scaled = held.tile([P, N], F32, name=f"scaled{k}")
+            nc.vector.tensor_tensor(scaled[:], table[k][:].indirect(offsets[:]), root_mean[:], MULT)
+            squares = held.tile([P, N], BF16, name=f"squares{k}")
+            nc.scalar.activation(squares[:], scaled[:], ACT.Square)
+            nc.tensor.matmul(mean_ps[:], ones[:], squares[:], start=(k == 0), stop=(k == KB - 1))
+        r = held.tile([P, N], F32, name="r")
+        nc.scalar.activation(r[:], mean_ps[:], ACT.Abs_reciprocal_sqrt)
+
+        gained = [held.tile([P, N], F32, name=f"gained{k}") for k in range(KB)]
+        for k in range(KB):
+            nc.vector.tensor_tensor(gained[k][:], table[k][:].indirect(offsets[:]), gain_cols[k][:], MULT)
+        hidden = [held.tile([P, N], BF16, name=f"hidden{k}") for k in range(KB)]
+        for k in range(KB):
+            nc.vector.tensor_tensor(hidden[k][:], gained[k][:], r[:], MULT)
+
+        logits = [psum.tile([P, N], F32, name=f"logits{m}") for m in range(MB)]
+        for k in range(KB):
+            for m in range(MB):
+                nc.tensor.matmul(
+                    logits[m][:], w_sb[:, k, m * P : (m + 1) * P], hidden[k][:],
+                    start=(k == 0), stop=(k == KB - 1),
+                )
+        for m in range(MB):
+            rows = held.tile([P, N], F32, name=f"rows{m}")
+            if m % 2 == 0:
+                nc.scalar.activation(rows[:], logits[m][:], ACT.Identity, bias=bias_sb[:, m : m + 1])
+            else:
+                nc.vector.tensor_scalar_add(rows[:], logits[m][:], bias_sb[:, m : m + 1])
+            nc.sync.dma_start(out[m * P : (m + 1) * P, :], rows[:])

@@ -39,6 +39,8 @@ def tile_llama_mla_kernel(tc, embed, gain, w_head, b_head, offs, out):
         nc.vector.memset(ones[:], 1.0)
         root_mean = held.tile([P, N], F32, name="root_mean")
         nc.vector.memset(root_mean[:], 1.0 / math.sqrt(C))
+        scratch = held.tile([P, 1], F32, name="scratch")
+        nc.scalar.activation(scratch[:], root_mean[:, 0:1], ACT.Abs_reciprocal_sqrt)
         gain_cols = [held.tile([P, N], F32, name=f"gain_cols{k}") for k in range(KB)]
         for k in range(KB):
             nc.gpsimd.tensor_copy(gain_cols[k][:], gain_sb[:, k : k + 1].to_broadcast([P, N]))

@@ -26,8 +26,8 @@ def tile_llama_mla_kernel(tc, embed, gain, w_head, b_head, offs, out):
 
         embed_blocks = embed.rearrange("(p k) s -> k p s", k=KB)
         table = [held.tile([P, S], F32, name=f"table{k}") for k in range(KB)]
-        nc.sync.dma_start(table[0][:], embed_blocks[0])
-        nc.scalar.dma_start(table[1][:], embed_blocks[1])
+        for k in range(KB):
+            nc.sync.dma_start(table[k][:], embed_blocks[k])
 
         w_sb = held.tile([P, KB, S], BF16, name="w_sb")
         nc.sync.dma_start(w_sb[:], w_head.rearrange("(p k) v -> p k v", k=KB))

@@ -7,6 +7,8 @@ C, S, N = 256, 512, 256
 KB = C // P
 MB = S // P
 FLOPS = 2 * C * S * N
+WARM_LOADS = 8
+WARM_NORM = 2
 
 F32, BF16, U16 = mybir.dt.float32, mybir.dt.bfloat16, mybir.dt.uint16
 MULT = mybir.AluOpType.mult
@@ -26,8 +28,8 @@ def tile_llama_mla_kernel(tc, embed, gain, w_head, b_head, offs, out):
 
         embed_blocks = embed.rearrange("(p k) s -> k p s", k=KB)
         table = [held.tile([P, S], F32, name=f"table{k}") for k in range(KB)]
-        for k in range(KB):
-            nc.sync.dma_start(table[k][:], embed_blocks[k])
+        nc.sync.dma_start(table[0][:], embed_blocks[0])
+        nc.scalar.dma_start(table[1][:], embed_blocks[1])
 
         w_sb = held.tile([P, KB, S], BF16, name="w_sb")
         nc.sync.dma_start(w_sb[:], w_head.rearrange("(p k) v -> p k v", k=KB))
@@ -39,6 +41,11 @@ def tile_llama_mla_kernel(tc, embed, gain, w_head, b_head, offs, out):
         nc.vector.memset(ones[:], 1.0)
         root_mean = held.tile([P, N], F32, name="root_mean")
         nc.vector.memset(root_mean[:], 1.0 / math.sqrt(C))
+        warm_in = held.tile([P, S], BF16, name="warm_in")
+        nc.gpsimd.memset(warm_in[:], 0.0)
+        warm_ps = psum.tile([P, S], F32, name="warm_ps")
+        for i in range(WARM_LOADS):
+            nc.tensor.matmul(warm_ps[:], ones[:], warm_in[:], start=True, stop=True)
         scratch = held.tile([P, 1], F32, name="scratch")
         nc.scalar.activation(scratch[:], root_mean[:, 0:1], ACT.Abs_reciprocal_sqrt)
         gain_cols = [held.tile([P, N], F32, name=f"gain_cols{k}") for k in range(KB)]
@@ -52,6 +59,8 @@ def tile_llama_mla_kernel(tc, embed, gain, w_head, b_head, offs, out):
             squares = held.tile([P, N], BF16, name=f"squares{k}")
             nc.scalar.activation(squares[:], scaled[:], ACT.Square)
             nc.tensor.matmul(mean_ps[:], ones[:], squares[:], start=(k == 0), stop=(k == KB - 1))
+        for i in range(WARM_NORM):
+            nc.tensor.matmul(warm_ps[:], ones[:], warm_in[:], start=True, stop=True)
         r = held.tile([P, N], F32, name="r")
         nc.scalar.activation(r[:], mean_ps[:], ACT.Abs_reciprocal_sqrt)
 

@@ -50,7 +50,7 @@ def tile_llama_mla_kernel(tc, embed, gain, w_head, b_head, offs, out):
         nc.scalar.activation(scratch[:], root_mean[:, 0:1], ACT.Abs_reciprocal_sqrt)
         gain_cols = [held.tile([P, N], F32, name=f"gain_cols{k}") for k in range(KB)]
         for k in range(KB):
-            nc.gpsimd.tensor_copy(gain_cols[k][:], gain_sb[:, k : k + 1].to_broadcast([P, N]))
+            nc.scalar.copy(gain_cols[k][:], gain_sb[:, k : k + 1].to_broadcast([P, N]))
 
         mean_ps = psum.tile([P, N], F32, name="mean_ps")
         for k in range(KB):

@@ -6,8 +6,10 @@ P = 128
 C, S, N = 256, 512, 256
 KB = C // P
 MB = S // P
+HALVES = 2
+HN = N // HALVES
 FLOPS = 2 * C * S * N
-WARM_LOADS = 8
+WARM_LOADS = 6
 WARM_NORM = 2
 
 F32, BF16, U16 = mybir.dt.float32, mybir.dt.bfloat16, mybir.dt.uint16
@@ -52,24 +54,31 @@ def tile_llama_mla_kernel(tc, embed, gain, w_head, b_head, offs, out):
         for k in range(KB):
             nc.scalar.copy(gain_cols[k][:], gain_sb[:, k : k + 1].to_broadcast([P, N]))
 
-        mean_ps = psum.tile([P, N], F32, name="mean_ps")
-        for k in range(KB):
-            scaled = held.tile([P, N], F32, name=f"scaled{k}")
-            nc.vector.tensor_tensor(scaled[:], table[k][:].indirect(offsets[:]), root_mean[:], MULT)
-            squares = held.tile([P, N], BF16, name=f"squares{k}")
-            nc.scalar.activation(squares[:], scaled[:], ACT.Square)
-            nc.tensor.matmul(mean_ps[:], ones[:], squares[:], start=(k == 0), stop=(k == KB - 1))
+        scaled = [held.tile([P, N], F32, name=f"scaled{k}") for k in range(KB)]
+        squares = [held.tile([P, N], BF16, name=f"squares{k}") for k in range(KB)]
+        r = held.tile([P, N], F32, name="r")
+        for h in range(HALVES):
+            cols = slice(h * HN, (h + 1) * HN)
+            half_list = offsets[:, h * (HN // 16) : (h + 1) * (HN // 16)]
+            mean_ps = psum.tile([P, HN], F32, name=f"mean_ps{h}")
+            for k in range(KB):
+                nc.vector.tensor_tensor(
+                    scaled[k][:, cols], table[k][:].indirect(half_list), root_mean[:, cols], MULT
+                )
+                nc.scalar.activation(squares[k][:, cols], scaled[k][:, cols], ACT.Square)
+                nc.tensor.matmul(mean_ps[:], ones[:], squares[k][:, cols], start=(k == 0), stop=(k == KB - 1))
+            nc.scalar.activation(r[:, cols], mean_ps[:], ACT.Abs_reciprocal_sqrt)
         for i in range(WARM_NORM):
             nc.tensor.matmul(warm_ps[:], ones[:], warm_in[:], start=True, stop=True)
-        r = held.tile([P, N], F32, name="r")
-        nc.scalar.activation(r[:], mean_ps[:], ACT.Abs_reciprocal_sqrt)
 
         gained = [held.tile([P, N], F32, name=f"gained{k}") for k in range(KB)]
         for k in range(KB):
             nc.vector.tensor_tensor(gained[k][:], table[k][:].indirect(offsets[:]), gain_cols[k][:], MULT)
         hidden = [held.tile([P, N], BF16, name=f"hidden{k}") for k in range(KB)]
         for k in range(KB):
-            nc.vector.tensor_tensor(hidden[k][:], gained[k][:], r[:], MULT)
+            for h in range(HALVES):
+                cols = slice(h * HN, (h + 1) * HN)
+                nc.vector.tensor_tensor(hidden[k][:, cols], gained[k][:, cols], r[:, cols], MULT)
 
         logits = [psum.tile([P, N], F32, name=f"logits{m}") for m in range(MB)]
         for k in range(KB):

@@ -54,20 +54,20 @@ def tile_llama_mla_kernel(tc, embed, gain, w_head, b_head, offs, out):
         for k in range(KB):
             nc.scalar.copy(gain_cols[k][:], gain_sb[:, k : k + 1].to_broadcast([P, N]))
 
-        scaled = [held.tile([P, N], F32, name=f"scaled{k}") for k in range(KB)]
-        squares = [held.tile([P, N], BF16, name=f"squares{k}") for k in range(KB)]
+        halves = [slice(h * HN, (h + 1) * HN) for h in range(HALVES)]
+        mean_ps = [psum.tile([P, HN], F32, name=f"mean_ps{h}") for h in range(HALVES)]
+        for k in range(KB):
+            scaled = held.tile([P, N], F32, name=f"scaled{k}")
+            nc.vector.tensor_tensor(scaled[:], table[k][:].indirect(offsets[:]), root_mean[:], MULT)
+            squares = held.tile([P, N], BF16, name=f"squares{k}")
+            for h in range(HALVES):
+                nc.scalar.activation(squares[:, halves[h]], scaled[:, halves[h]], ACT.Square)
+                nc.tensor.matmul(
+                    mean_ps[h][:], ones[:], squares[:, halves[h]], start=(k == 0), stop=(k == KB - 1)
+                )
         r = held.tile([P, N], F32, name="r")
         for h in range(HALVES):
-            cols = slice(h * HN, (h + 1) * HN)
-            half_list = offsets[:, h * (HN // 16) : (h + 1) * (HN // 16)]
-            mean_ps = psum.tile([P, HN], F32, name=f"mean_ps{h}")
-            for k in range(KB):
-                nc.vector.tensor_tensor(
-                    scaled[k][:, cols], table[k][:].indirect(half_list), root_mean[:, cols], MULT
-                )
-                nc.scalar.activation(squares[k][:, cols], scaled[k][:, cols], ACT.Square)
-                nc.tensor.matmul(mean_ps[:], ones[:], squares[k][:, cols], start=(k == 0), stop=(k == KB - 1))
-            nc.scalar.activation(r[:, cols], mean_ps[:], ACT.Abs_reciprocal_sqrt)
+            nc.scalar.activation(r[:, halves[h]], mean_ps[h][:], ACT.Abs_reciprocal_sqrt)
         for i in range(WARM_NORM):
             nc.tensor.matmul(warm_ps[:], ones[:], warm_in[:], start=True, stop=True)
 
@@ -76,9 +76,7 @@ def tile_llama_mla_kernel(tc, embed, gain, w_head, b_head, offs, out):
             nc.vector.tensor_tensor(gained[k][:], table[k][:].indirect(offsets[:]), gain_cols[k][:], MULT)
         hidden = [held.tile([P, N], BF16, name=f"hidden{k}") for k in range(KB)]
         for k in range(KB):
-            for h in range(HALVES):
-                cols = slice(h * HN, (h + 1) * HN)
-                nc.vector.tensor_tensor(hidden[k][:, cols], gained[k][:, cols], r[:, cols], MULT)
+            nc.vector.tensor_tensor(hidden[k][:], gained[k][:], r[:], MULT)
 
         logits = [psum.tile([P, N], F32, name=f"logits{m}") for m in range(MB)]
         for k in range(KB):

@@ -33,12 +33,6 @@ def tile_llama_mla_kernel(tc, embed, gain, w_head, b_head, offs, out):
         nc.sync.dma_start(table[0][:], embed_blocks[0])
         nc.scalar.dma_start(table[1][:], embed_blocks[1])
 
-        w_sb = held.tile([P, KB, S], BF16, name="w_sb")
-        nc.sync.dma_start(w_sb[:], w_head.rearrange("(p k) v -> p k v", k=KB))
-        bias_sb = held.tile([P, MB], F32, name="bias_sb")
-        with nc.allow_non_contiguous_dma(reason="512 bias values, one to a partition"):
-            nc.scalar.dma_start(bias_sb[:], b_head.rearrange("(m p) o -> p (m o)", p=P))
-
         ones = held.tile([P, P], BF16, name="ones")
         nc.vector.memset(ones[:], 1.0)
         root_mean = held.tile([P, N], F32, name="root_mean")
@@ -50,6 +44,11 @@ def tile_llama_mla_kernel(tc, embed, gain, w_head, b_head, offs, out):
             nc.tensor.matmul(warm_ps[:], ones[:], warm_in[:], start=True, stop=True)
         scratch = held.tile([P, 1], F32, name="scratch")
         nc.scalar.activation(scratch[:], root_mean[:, 0:1], ACT.Abs_reciprocal_sqrt)
+        w_sb = held.tile([P, KB, S], BF16, name="w_sb")
+        nc.scalar.dma_start(w_sb[:], w_head.rearrange("(p k) v -> p k v", k=KB))
+        bias_sb = held.tile([P, MB], F32, name="bias_sb")
+        with nc.allow_non_contiguous_dma(reason="512 bias values, one to a partition"):
+            nc.scalar.dma_start(bias_sb[:], b_head.rearrange("(m p) o -> p (m o)", p=P))
         gain_cols = [held.tile([P, N], F32, name=f"gain_cols{k}") for k in range(KB)]
         for k in range(KB):
             nc.scalar.copy(gain_cols[k][:], gain_sb[:, k : k + 1].to_broadcast([P, N]))

@@ -78,12 +78,13 @@ def tile_llama_mla_kernel(tc, embed, gain, w_head, b_head, offs, out):
             nc.vector.tensor_tensor(hidden[k][:], gained[k][:], r[:], MULT)
 
         logits = [psum.tile([P, N], F32, name=f"logits{m}") for m in range(MB)]
-        for k in range(KB):
-            for m in range(MB):
-                nc.tensor.matmul(
-                    logits[m][:], w_sb[:, k, m * P : (m + 1) * P], hidden[k][:],
-                    start=(k == 0), stop=(k == KB - 1),
-                )
+        for pair in range(0, MB, 2):
+            for k in range(KB):
+                for m in (pair, pair + 1):
+                    nc.tensor.matmul(
+                        logits[m][:], w_sb[:, k, m * P : (m + 1) * P], hidden[k][:],
+                        start=(k == 0), stop=(k == KB - 1),
+                    )
         for m in range(MB):
             rows = held.tile([P, N], F32, name=f"rows{m}")
             if m % 2 == 0:

@@ -1,5 +1,3 @@
-import math
-
 import concourse.mybir as mybir
 
 P = 128
@@ -8,12 +6,13 @@ KB = C // P
 MB = S // P
 HALVES = 2
 HN = N // HALVES
+TINY = 2.0**-30
 FLOPS = 2 * C * S * N
 WARM_LOADS = 6
-WARM_NORM = 2
 
 F32, BF16, U16 = mybir.dt.float32, mybir.dt.bfloat16, mybir.dt.uint16
-MULT = mybir.AluOpType.mult
+ADD, MULT = mybir.AluOpType.add, mybir.AluOpType.mult
+IS_GT = mybir.AluOpType.is_gt
 ACT = mybir.ActivationFunctionType
 
 
@@ -32,63 +31,64 @@ def tile_llama_mla_kernel(tc, embed, gain, w_head, b_head, offs, out):
         table = [held.tile([P, S], F32, name=f"table{k}") for k in range(KB)]
         nc.sync.dma_start(table[0][:], embed_blocks[0])
         nc.scalar.dma_start(table[1][:], embed_blocks[1])
+        w_sb = held.tile([P, KB, S], BF16, name="w_sb")
+        nc.sync.dma_start(w_sb[:], w_head.rearrange("(p k) v -> p k v", k=KB))
 
         ones = held.tile([P, P], BF16, name="ones")
         nc.vector.memset(ones[:], 1.0)
-        root_mean = held.tile([P, N], F32, name="root_mean")
-        nc.vector.memset(root_mean[:], 1.0 / math.sqrt(C))
+        tiny_sq = held.tile([P, N], F32, name="tiny_sq")
+        nc.vector.memset(tiny_sq[:], TINY * TINY)
+        one = held.tile([P, 1], F32, name="one")
+        nc.vector.memset(one[:], 1.0)
         warm_in = held.tile([P, S], BF16, name="warm_in")
         nc.gpsimd.memset(warm_in[:], 0.0)
         warm_ps = psum.tile([P, S], F32, name="warm_ps")
         for i in range(WARM_LOADS):
             nc.tensor.matmul(warm_ps[:], ones[:], warm_in[:], start=True, stop=True)
         scratch = held.tile([P, 1], F32, name="scratch")
-        nc.scalar.activation(scratch[:], root_mean[:, 0:1], ACT.Abs_reciprocal_sqrt)
-        w_sb = held.tile([P, KB, S], BF16, name="w_sb")
-        nc.scalar.dma_start(w_sb[:], w_head.rearrange("(p k) v -> p k v", k=KB))
+        nc.scalar.activation(scratch[:], one[:], ACT.Abs_reciprocal_sqrt)
         bias_sb = held.tile([P, MB], F32, name="bias_sb")
         with nc.allow_non_contiguous_dma(reason="512 bias values, one to a partition"):
             nc.scalar.dma_start(bias_sb[:], b_head.rearrange("(m p) o -> p (m o)", p=P))
+        gain_sq = held.tile([P, KB], F32, name="gain_sq")
+        nc.vector.tensor_tensor(gain_sq[:], gain_sb[:], gain_sb[:], MULT)
         gain_cols = [held.tile([P, N], F32, name=f"gain_cols{k}") for k in range(KB)]
         for k in range(KB):
-            nc.scalar.copy(gain_cols[k][:], gain_sb[:, k : k + 1].to_broadcast([P, N]))
+            nc.vector.tensor_scalar(
+                gain_cols[k][:], tiny_sq[:], gain_sq[:, k : k + 1], gain_sb[:, k : k + 1], IS_GT, ADD
+            )
+        inv_gain = held.tile([P, KB], F32, name="inv_gain")
+        for k in range(KB):
+            nc.vector.reciprocal(inv_gain[:, k : k + 1], gain_cols[k][:, 0:1])
 
         halves = [slice(h * HN, (h + 1) * HN) for h in range(HALVES)]
-        mean_ps = [psum.tile([P, HN], F32, name=f"mean_ps{h}") for h in range(HALVES)]
+        sum_ps = [psum.tile([P, HN], F32, name=f"sum_ps{h}") for h in range(HALVES)]
+        logits = [psum.tile([P, N], F32, name=f"logits{m}") for m in range(MB)]
         for k in range(KB):
-            scaled = held.tile([P, N], F32, name=f"scaled{k}")
-            nc.vector.tensor_tensor(scaled[:], table[k][:].indirect(offsets[:]), root_mean[:], MULT)
+            first, last = k == 0, k == KB - 1
+            gained = held.tile([P, N], F32, name=f"gained{k}")
+            nc.vector.tensor_tensor(gained[:], table[k][:].indirect(offsets[:]), gain_cols[k][:], MULT)
+            hidden = held.tile([P, N], BF16, name=f"hidden{k}")
+            nc.vector.tensor_scalar(
+                hidden[:], gained[:], inv_gain[:, k : k + 1], gain_sb[:, k : k + 1], MULT, MULT
+            )
             squares = held.tile([P, N], BF16, name=f"squares{k}")
-            for h in range(HALVES):
-                nc.scalar.activation(squares[:, halves[h]], scaled[:, halves[h]], ACT.Square)
+            for half, total in zip(halves, sum_ps):
+                nc.scalar.activation(
+                    squares[:, half], gained[:, half], ACT.Square, scale=inv_gain[:, k : k + 1]
+                )
+                nc.tensor.matmul(total[:], ones[:], squares[:, half], start=first, stop=last)
+            for m in range(MB):
                 nc.tensor.matmul(
-                    mean_ps[h][:], ones[:], squares[:, halves[h]], start=(k == 0), stop=(k == KB - 1)
+                    logits[m][:], w_sb[:, k, m * P : (m + 1) * P], hidden[:], start=first, stop=last
                 )
         r = held.tile([P, N], F32, name="r")
-        for h in range(HALVES):
-            nc.scalar.activation(r[:, halves[h]], mean_ps[h][:], ACT.Abs_reciprocal_sqrt)
-        for i in range(WARM_NORM):
-            nc.tensor.matmul(warm_ps[:], ones[:], warm_in[:], start=True, stop=True)
+        for half, total in zip(halves, sum_ps):
+            nc.scalar.activation(r[:, half], total[:], ACT.Abs_reciprocal_sqrt, scale=1.0 / C)
 
-        gained = [held.tile([P, N], F32, name=f"gained{k}") for k in range(KB)]
-        for k in range(KB):
-            nc.vector.tensor_tensor(gained[k][:], table[k][:].indirect(offsets[:]), gain_cols[k][:], MULT)
-        hidden = [held.tile([P, N], BF16, name=f"hidden{k}") for k in range(KB)]
-        for k in range(KB):
-            nc.vector.tensor_tensor(hidden[k][:], gained[k][:], r[:], MULT)
-
-        logits = [psum.tile([P, N], F32, name=f"logits{m}") for m in range(MB)]
-        for pair in range(0, MB, 2):
-            for k in range(KB):
-                for m in (pair, pair + 1):
-                    nc.tensor.matmul(
-                        logits[m][:], w_sb[:, k, m * P : (m + 1) * P], hidden[k][:],
-                        start=(k == 0), stop=(k == KB - 1),
-                    )
         for m in range(MB):
+            normed = held.tile([P, N], F32, name=f"normed{m}")
+            nc.vector.tensor_tensor(normed[:], logits[m][:], r[:], MULT)
             rows = held.tile([P, N], F32, name=f"rows{m}")
-            if m % 2 == 0:
-                nc.scalar.activation(rows[:], logits[m][:], ACT.Identity, bias=bias_sb[:, m : m + 1])
-            else:
-                nc.vector.tensor_scalar_add(rows[:], logits[m][:], bias_sb[:, m : m + 1])
+            nc.scalar.activation(rows[:], normed[:], ACT.Identity, bias=bias_sb[:, m : m + 1])
             nc.sync.dma_start(out[m * P : (m + 1) * P, :], rows[:])

@@ -36,7 +36,7 @@ def tile_llama_mla_kernel(tc, embed, gain, w_head, b_head, offs, out):
 
         ones = held.tile([P, P], BF16, name="ones")
         nc.vector.memset(ones[:], 1.0)
-        tiny_sq = held.tile([P, N], F32, name="tiny_sq")
+        tiny_sq = held.tile([P, HN], F32, name="tiny_sq")
         nc.vector.memset(tiny_sq[:], TINY * TINY)
         one = held.tile([P, 1], F32, name="one")
         nc.vector.memset(one[:], 1.0)
@@ -52,7 +52,7 @@ def tile_llama_mla_kernel(tc, embed, gain, w_head, b_head, offs, out):
             nc.scalar.dma_start(bias_sb[:], b_head.rearrange("(m p) o -> p (m o)", p=P))
         gain_sq = held.tile([P, KB], F32, name="gain_sq")
         nc.vector.tensor_tensor(gain_sq[:], gain_sb[:], gain_sb[:], MULT)
-        gain_cols = [held.tile([P, N], F32, name=f"gain_cols{k}") for k in range(KB)]
+        gain_cols = [held.tile([P, HN], F32, name=f"gain_cols{k}") for k in range(KB)]
         for k in range(KB):
             nc.vector.tensor_scalar(
                 gain_cols[k][:], tiny_sq[:], gain_sq[:, k : k + 1], gain_sb[:, k : k + 1], IS_GT, ADD
@@ -61,34 +61,39 @@ def tile_llama_mla_kernel(tc, embed, gain, w_head, b_head, offs, out):
         for k in range(KB):
             nc.vector.reciprocal(inv_gain[:, k : k + 1], gain_cols[k][:, 0:1])
 
-        halves = [slice(h * HN, (h + 1) * HN) for h in range(HALVES)]
-        sum_ps = [psum.tile([P, HN], F32, name=f"sum_ps{h}") for h in range(HALVES)]
-        logits = [psum.tile([P, N], F32, name=f"logits{m}") for m in range(MB)]
-        for k in range(KB):
-            first, last = k == 0, k == KB - 1
-            gained = held.tile([P, N], F32, name=f"gained{k}")
-            nc.vector.tensor_tensor(gained[:], table[k][:].indirect(offsets[:]), gain_cols[k][:], MULT)
-            hidden = held.tile([P, N], BF16, name=f"hidden{k}")
-            nc.vector.tensor_scalar(
-                hidden[:], gained[:], inv_gain[:, k : k + 1], gain_sb[:, k : k + 1], MULT, MULT
-            )
-            squares = held.tile([P, N], BF16, name=f"squares{k}")
-            for half, total in zip(halves, sum_ps):
-                nc.scalar.activation(
-                    squares[:, half], gained[:, half], ACT.Square, scale=inv_gain[:, k : k + 1]
+        out_blocks = out.rearrange("(m p) n -> p m n", p=P)
+        for h in range(HALVES):
+            tokens = slice(h * HN, (h + 1) * HN)
+            list_h = offsets[:, h * HN // 16 : (h + 1) * HN // 16]
+            sum_ps = psum.tile([P, HN], F32, name=f"sum_ps{h}")
+            hidden = [held.tile([P, HN], BF16, name=f"hidden{h}_{k}") for k in range(KB)]
+            for k in range(KB):
+                gained = held.tile([P, HN], F32, name=f"gained{h}_{k}")
+                nc.vector.tensor_tensor(gained[:], table[k][:].indirect(list_h), gain_cols[k][:], MULT)
+                nc.vector.tensor_scalar(
+                    hidden[k][:], gained[:], inv_gain[:, k : k + 1], gain_sb[:, k : k + 1], MULT, MULT
                 )
-                nc.tensor.matmul(total[:], ones[:], squares[:, half], start=first, stop=last)
-            for m in range(MB):
-                nc.tensor.matmul(
-                    logits[m][:], w_sb[:, k, m * P : (m + 1) * P], hidden[:], start=first, stop=last
-                )
-        r = held.tile([P, N], F32, name="r")
-        for half, total in zip(halves, sum_ps):
-            nc.scalar.activation(r[:, half], total[:], ACT.Abs_reciprocal_sqrt, scale=1.0 / C)
+                squares = held.tile([P, HN], BF16, name=f"squares{h}_{k}")
+                nc.scalar.activation(squares[:], gained[:], ACT.Square, scale=inv_gain[:, k : k + 1])
+                nc.tensor.matmul(sum_ps[:], ones[:], squares[:], start=(k == 0), stop=(k == KB - 1))
+            r = held.tile([P, HN], F32, name=f"r{h}")
+            nc.scalar.activation(r[:], sum_ps[:], ACT.Abs_reciprocal_sqrt, scale=1.0 / C)
 
-        for m in range(MB):
-            normed = held.tile([P, N], F32, name=f"normed{m}")
-            nc.vector.tensor_tensor(normed[:], logits[m][:], r[:], MULT)
-            rows = held.tile([P, N], F32, name=f"rows{m}")
-            nc.scalar.activation(rows[:], normed[:], ACT.Identity, bias=bias_sb[:, m : m + 1])
-            nc.sync.dma_start(out[m * P : (m + 1) * P, :], rows[:])
+            logits = psum.tile([P, MB, HN], F32, name=f"logits{h}")
+            for m in range(MB):
+                for k in range(KB):
+                    nc.tensor.matmul(
+                        logits[:, m, :], w_sb[:, k, m * P : (m + 1) * P], hidden[k][:],
+                        start=(k == 0), stop=(k == KB - 1),
+                    )
+            for pair in range(0, MB, 2):
+                normed = held.tile([P, 2, HN], F32, name=f"normed{h}_{pair}")
+                nc.vector.tensor_tensor(
+                    normed[:], logits[:, pair : pair + 2, :], r[:].unsqueeze(1).to_broadcast([P, 2, HN]), MULT
+                )
+                rows = held.tile([P, 2, HN], F32, name=f"rows{h}_{pair}")
+                for i in range(2):
+                    nc.scalar.activation(
+                        rows[:, i, :], normed[:, i, :], ACT.Identity, bias=bias_sb[:, pair + i : pair + i + 1]
+                    )
+                nc.sync.dma_start(out_blocks[:, pair : pair + 2, tokens], rows[:])

@@ -31,8 +31,6 @@ def tile_llama_mla_kernel(tc, embed, gain, w_head, b_head, offs, out):
         table = [held.tile([P, S], F32, name=f"table{k}") for k in range(KB)]
         nc.sync.dma_start(table[0][:], embed_blocks[0])
         nc.scalar.dma_start(table[1][:], embed_blocks[1])
-        w_sb = held.tile([P, KB, S], BF16, name="w_sb")
-        nc.sync.dma_start(w_sb[:], w_head.rearrange("(p k) v -> p k v", k=KB))
 
         ones = held.tile([P, P], BF16, name="ones")
         nc.vector.memset(ones[:], 1.0)
@@ -40,11 +38,13 @@ def tile_llama_mla_kernel(tc, embed, gain, w_head, b_head, offs, out):
         nc.vector.memset(tiny_sq[:], TINY * TINY)
         one = held.tile([P, 1], F32, name="one")
         nc.vector.memset(one[:], 1.0)
-        warm_in = held.tile([P, S], BF16, name="warm_in")
-        nc.gpsimd.memset(warm_in[:], 0.0)
-        warm_ps = psum.tile([P, S], F32, name="warm_ps")
+        w_sb = held.tile([P, KB, S], BF16, name="w_sb")
+        nc.gpsimd.dma_start(w_sb[:], w_head.rearrange("(p k) v -> p k v", k=KB))
+        warm_ps = psum.tile([P, S // P, P], F32, name="warm_ps")
         for i in range(WARM_LOADS):
-            nc.tensor.matmul(warm_ps[:], ones[:], warm_in[:], start=True, stop=True)
+            nc.tensor.matmul(
+                warm_ps[:], ones[:], ones[:].unsqueeze(1).to_broadcast([P, S // P, P]), start=True, stop=True
+            )
         scratch = held.tile([P, 1], F32, name="scratch")
         nc.scalar.activation(scratch[:], one[:], ACT.Abs_reciprocal_sqrt)
         bias_sb = held.tile([P, MB], F32, name="bias_sb")
@@ -79,17 +79,18 @@ def tile_llama_mla_kernel(tc, embed, gain, w_head, b_head, offs, out):
             r = held.tile([P, HN], F32, name=f"r{h}")
             nc.scalar.activation(r[:], sum_ps[:], ACT.Abs_reciprocal_sqrt, scale=1.0 / C)
 
-            logits = psum.tile([P, MB, HN], F32, name=f"logits{h}")
-            for m in range(MB):
-                for k in range(KB):
-                    nc.tensor.matmul(
-                        logits[:, m, :], w_sb[:, k, m * P : (m + 1) * P], hidden[k][:],
-                        start=(k == 0), stop=(k == KB - 1),
-                    )
             for pair in range(0, MB, 2):
+                logits = psum.tile([P, 2, HN], F32, name=f"logits{h}_{pair}")
+                for i in range(2):
+                    m = pair + i
+                    for k in range(KB):
+                        nc.tensor.matmul(
+                            logits[:, i, :], w_sb[:, k, m * P : (m + 1) * P], hidden[k][:],
+                            start=(k == 0), stop=(k == KB - 1),
+                        )
                 normed = held.tile([P, 2, HN], F32, name=f"normed{h}_{pair}")
                 nc.vector.tensor_tensor(
-                    normed[:], logits[:, pair : pair + 2, :], r[:].unsqueeze(1).to_broadcast([P, 2, HN]), MULT
+                    normed[:], logits[:], r[:].unsqueeze(1).to_broadcast([P, 2, HN]), MULT
                 )
                 rows = held.tile([P, 2, HN], F32, name=f"rows{h}_{pair}")
                 for i in range(2):

@@ -48,8 +48,7 @@ def tile_llama_mla_kernel(tc, embed, gain, w_head, b_head, offs, out):
         scratch = held.tile([P, 1], F32, name="scratch")
         nc.scalar.activation(scratch[:], one[:], ACT.Abs_reciprocal_sqrt)
         bias_sb = held.tile([P, MB], F32, name="bias_sb")
-        with nc.allow_non_contiguous_dma(reason="512 bias values, one to a partition"):
-            nc.scalar.dma_start(bias_sb[:], b_head.rearrange("(m p) o -> p (m o)", p=P))
+        nc.scalar.dma_start(bias_sb[:], b_head.rearrange("(p m) o -> p (m o)", m=MB))
         gain_sq = held.tile([P, KB], F32, name="gain_sq")
         nc.vector.tensor_tensor(gain_sq[:], gain_sb[:], gain_sb[:], MULT)
         gain_cols = [held.tile([P, HN], F32, name=f"gain_cols{k}") for k in range(KB)]
@@ -61,7 +60,8 @@ def tile_llama_mla_kernel(tc, embed, gain, w_head, b_head, offs, out):
         for k in range(KB):
             nc.vector.reciprocal(inv_gain[:, k : k + 1], gain_cols[k][:, 0:1])
 
-        out_blocks = out.rearrange("(m p) n -> p m n", p=P)
+        out_blocks = out.rearrange("(p m) n -> p m n", m=MB)
+        w_blocks = w_sb[:].rearrange("p k (q m) -> p k m q", m=MB)
         for h in range(HALVES):
             tokens = slice(h * HN, (h + 1) * HN)
             list_h = offsets[:, h * HN // 16 : (h + 1) * HN // 16]
@@ -85,7 +85,7 @@ def tile_llama_mla_kernel(tc, embed, gain, w_head, b_head, offs, out):
                     m = pair + i
                     for k in range(KB):
                         nc.tensor.matmul(
-                            logits[:, i, :], w_sb[:, k, m * P : (m + 1) * P], hidden[k][:],
+                            logits[:, i, :], w_blocks[:, k, m, :], hidden[k][:],
                             start=(k == 0), stop=(k == KB - 1),
                         )
                 normed = held.tile([P, 2, HN], F32, name=f"normed{h}_{pair}")

@@ -94,7 +94,9 @@ def tile_llama_mla_kernel(tc, embed, gain, w_head, b_head, offs, out):
                 )
                 rows = held.tile([P, 2, HN], F32, name=f"rows{h}_{pair}")
                 for i in range(2):
-                    nc.scalar.activation(
-                        rows[:, i, :], normed[:, i, :], ACT.Identity, bias=bias_sb[:, pair + i : pair + i + 1]
-                    )
+                    bias = bias_sb[:, pair + i : pair + i + 1]
+                    if h == HALVES - 1 and pair == MB - 2:
+                        nc.vector.tensor_scalar_add(rows[:, i, :], normed[:, i, :], bias)
+                    else:
+                        nc.scalar.activation(rows[:, i, :], normed[:, i, :], ACT.Identity, bias=bias)
                 nc.sync.dma_start(out_blocks[:, pair : pair + 2, tokens], rows[:])

@@ -62,6 +62,7 @@ def tile_llama_mla_kernel(tc, embed, gain, w_head, b_head, offs, out):
 
         out_blocks = out.rearrange("(p m) n -> p m n", m=MB)
         w_blocks = w_sb[:].rearrange("p k (q m) -> p k m q", m=MB)
+        rows = [held.tile([P, 2, N], F32, name=f"rows{pair}") for pair in range(0, MB, 2)]
         for h in range(HALVES):
             tokens = slice(h * HN, (h + 1) * HN)
             list_h = offsets[:, h * HN // 16 : (h + 1) * HN // 16]
@@ -92,11 +93,11 @@ def tile_llama_mla_kernel(tc, embed, gain, w_head, b_head, offs, out):
                 nc.vector.tensor_tensor(
                     normed[:], logits[:], r[:].unsqueeze(1).to_broadcast([P, 2, HN]), MULT
                 )
-                rows = held.tile([P, 2, HN], F32, name=f"rows{h}_{pair}")
                 for i in range(2):
                     bias = bias_sb[:, pair + i : pair + i + 1]
                     if h == HALVES - 1 and pair == MB - 2:
-                        nc.vector.tensor_scalar_add(rows[:, i, :], normed[:, i, :], bias)
+                        nc.vector.tensor_scalar_add(rows[pair // 2][:, i, tokens], normed[:, i, :], bias)
                     else:
-                        nc.scalar.activation(rows[:, i, :], normed[:, i, :], ACT.Identity, bias=bias)
-                nc.sync.dma_start(out_blocks[:, pair : pair + 2, tokens], rows[:])
+                        nc.scalar.activation(rows[pair // 2][:, i, tokens], normed[:, i, :], ACT.Identity, bias=bias)
+                if h == HALVES - 1:
+                    nc.sync.dma_start(out_blocks[:, pair : pair + 2, :], rows[pair // 2][:])

@@ -95,9 +95,10 @@ def tile_llama_mla_kernel(tc, embed, gain, w_head, b_head, offs, out):
                 )
                 for i in range(2):
                     bias = bias_sb[:, pair + i : pair + i + 1]
-                    if h == HALVES - 1 and pair == MB - 2:
+                    if h == HALVES - 1 and i == 1:
                         nc.vector.tensor_scalar_add(rows[pair // 2][:, i, tokens], normed[:, i, :], bias)
                     else:
                         nc.scalar.activation(rows[pair // 2][:, i, tokens], normed[:, i, :], ACT.Identity, bias=bias)
                 if h == HALVES - 1:
-                    nc.sync.dma_start(out_blocks[:, pair : pair + 2, :], rows[pair // 2][:])
+                    store_queue = nc.scalar if pair == 0 else nc.sync
+                    store_queue.dma_start(out_blocks[:, pair : pair + 2, :], rows[pair // 2][:])

@@ -30,11 +30,11 @@ def tile_llama_mla_kernel(tc, embed, gain, w_head, b_head, offs, out):
         embed_blocks = embed.rearrange("(p k) s -> k p s", k=KB)
         table = [held.tile([P, S], F32, name=f"table{k}") for k in range(KB)]
         nc.sync.dma_start(table[0][:], embed_blocks[0])
-        nc.scalar.dma_start(table[1][:], embed_blocks[1])
+        nc.sync.dma_start(table[1][:], embed_blocks[1])
 
         ones = held.tile([P, P], BF16, name="ones")
         nc.vector.memset(ones[:], 1.0)
-        tiny_sq = held.tile([P, HN], F32, name="tiny_sq")
+        tiny_sq = held.tile([P, N], F32, name="tiny_sq")
         nc.vector.memset(tiny_sq[:], TINY * TINY)
         one = held.tile([P, 1], F32, name="one")
         nc.vector.memset(one[:], 1.0)
@@ -51,7 +51,7 @@ def tile_llama_mla_kernel(tc, embed, gain, w_head, b_head, offs, out):
         nc.scalar.dma_start(bias_sb[:], b_head.rearrange("(p m) o -> p (m o)", m=MB))
         gain_sq = held.tile([P, KB], F32, name="gain_sq")
         nc.vector.tensor_tensor(gain_sq[:], gain_sb[:], gain_sb[:], MULT)
-        gain_cols = [held.tile([P, HN], F32, name=f"gain_cols{k}") for k in range(KB)]
+        gain_cols = [held.tile([P, N], F32, name=f"gain_cols{k}") for k in range(KB)]
         for k in range(KB):
             nc.vector.tensor_scalar(
                 gain_cols[k][:], tiny_sq[:], gain_sq[:, k : k + 1], gain_sb[:, k : k + 1], IS_GT, ADD
@@ -62,23 +62,34 @@ def tile_llama_mla_kernel(tc, embed, gain, w_head, b_head, offs, out):
 
         out_blocks = out.rearrange("(p m) n -> p m n", m=MB)
         w_blocks = w_sb[:].rearrange("p k (q m) -> p k m q", m=MB)
+        sums = [psum.tile([P, HN], F32, name=f"sum_ps{h}") for h in range(HALVES)]
+
+        def look_up(k, tokens, halves):
+            width = tokens.stop - tokens.start
+            gained = held.tile([P, width], F32, name=f"gained{k}_{tokens.start}")
+            list_part = offsets[:, tokens.start // 16 : tokens.stop // 16]
+            nc.vector.tensor_tensor(
+                gained[:], table[k][:].indirect(list_part), gain_cols[k][:, :width], MULT
+            )
+            hidden = held.tile([P, width], BF16, name=f"hidden{k}_{tokens.start}")
+            nc.vector.tensor_scalar(
+                hidden[:], gained[:], inv_gain[:, k : k + 1], gain_sb[:, k : k + 1], MULT, MULT
+            )
+            squares = held.tile([P, width], BF16, name=f"squares{k}_{tokens.start}")
+            nc.scalar.activation(squares[:], gained[:], ACT.Square, scale=inv_gain[:, k : k + 1])
+            for i, h in enumerate(halves):
+                nc.tensor.matmul(
+                    sums[h][:], ones[:], squares[:, i * HN : (i + 1) * HN], start=(k == 0), stop=(k == KB - 1)
+                )
+            return hidden
+
         rows = [held.tile([P, 2, N], F32, name=f"rows{pair}") for pair in range(0, MB, 2)]
+        hidden0 = look_up(0, slice(0, N), range(HALVES))
         for h in range(HALVES):
             tokens = slice(h * HN, (h + 1) * HN)
-            list_h = offsets[:, h * HN // 16 : (h + 1) * HN // 16]
-            sum_ps = psum.tile([P, HN], F32, name=f"sum_ps{h}")
-            hidden = [held.tile([P, HN], BF16, name=f"hidden{h}_{k}") for k in range(KB)]
-            for k in range(KB):
-                gained = held.tile([P, HN], F32, name=f"gained{h}_{k}")
-                nc.vector.tensor_tensor(gained[:], table[k][:].indirect(list_h), gain_cols[k][:], MULT)
-                nc.vector.tensor_scalar(
-                    hidden[k][:], gained[:], inv_gain[:, k : k + 1], gain_sb[:, k : k + 1], MULT, MULT
-                )
-                squares = held.tile([P, HN], BF16, name=f"squares{h}_{k}")
-                nc.scalar.activation(squares[:], gained[:], ACT.Square, scale=inv_gain[:, k : k + 1])
-                nc.tensor.matmul(sum_ps[:], ones[:], squares[:], start=(k == 0), stop=(k == KB - 1))
+            hidden = [hidden0[:, tokens], look_up(1, tokens, [h])[:]]
             r = held.tile([P, HN], F32, name=f"r{h}")
-            nc.scalar.activation(r[:], sum_ps[:], ACT.Abs_reciprocal_sqrt, scale=1.0 / C)
+            nc.scalar.activation(r[:], sums[h][:], ACT.Abs_reciprocal_sqrt, scale=1.0 / C)
 
             for pair in range(0, MB, 2):
                 logits = psum.tile([P, 2, HN], F32, name=f"logits{h}_{pair}")
@@ -86,7 +97,7 @@ def tile_llama_mla_kernel(tc, embed, gain, w_head, b_head, offs, out):
                     m = pair + i
                     for k in range(KB):
                         nc.tensor.matmul(
-                            logits[:, i, :], w_blocks[:, k, m, :], hidden[k][:],
+                            logits[:, i, :], w_blocks[:, k, m, :], hidden[k],
                             start=(k == 0), stop=(k == KB - 1),
                         )
                 normed = held.tile([P, 2, HN], F32, name=f"normed{h}_{pair}")

@@ -31,6 +31,8 @@ def tile_llama_mla_kernel(tc, embed, gain, w_head, b_head, offs, out):
         table = [held.tile([P, S], F32, name=f"table{k}") for k in range(KB)]
         nc.sync.dma_start(table[0][:], embed_blocks[0])
         nc.sync.dma_start(table[1][:], embed_blocks[1])
+        w_sb = held.tile([P, KB, S], BF16, name="w_sb")
+        nc.sync.dma_start(w_sb[:], w_head.rearrange("(p k) v -> p k v", k=KB))
 
         ones = held.tile([P, P], BF16, name="ones")
         nc.vector.memset(ones[:], 1.0)
@@ -38,8 +40,6 @@ def tile_llama_mla_kernel(tc, embed, gain, w_head, b_head, offs, out):
         nc.vector.memset(tiny_sq[:], TINY * TINY)
         one = held.tile([P, 1], F32, name="one")
         nc.vector.memset(one[:], 1.0)
-        w_sb = held.tile([P, KB, S], BF16, name="w_sb")
-        nc.gpsimd.dma_start(w_sb[:], w_head.rearrange("(p k) v -> p k v", k=KB))
         warm_ps = psum.tile([P, S // P, P], F32, name="warm_ps")
         for i in range(WARM_LOADS):
             nc.tensor.matmul(

import concourse.mybir as mybir

P = 128
C, S, N = 256, 512, 256
KB = C // P
MB = S // P
HALVES = 2
HN = N // HALVES
TINY = 2.0**-30
FLOPS = 2 * C * S * N
WARM_LOADS = 6

F32, BF16, U16 = mybir.dt.float32, mybir.dt.bfloat16, mybir.dt.uint16
ADD, MULT = mybir.AluOpType.add, mybir.AluOpType.mult
IS_GT = mybir.AluOpType.is_gt
ACT = mybir.ActivationFunctionType


def tile_llama_mla_kernel(tc, embed, gain, w_head, b_head, offs, out):
    nc = tc.nc
    with (
        tc.tile_pool(name="held", bufs=1) as held,
        tc.psum_pool(name="psum", bufs=1) as psum,
    ):
        offsets = held.tile([P, N // 16], U16, name="offsets")
        nc.sync.dma_start(offsets[:], offs)
        gain_sb = held.tile([P, KB], F32, name="gain_sb")
        nc.scalar.dma_start(gain_sb[:], gain.rearrange("(p k) o -> p (k o)", k=KB))

        embed_blocks = embed.rearrange("(p k) s -> k p s", k=KB)
        table = [held.tile([P, S], F32, name=f"table{k}") for k in range(KB)]
        nc.sync.dma_start(table[0][:], embed_blocks[0])
        nc.sync.dma_start(table[1][:], embed_blocks[1])
        w_sb = held.tile([P, KB, S], BF16, name="w_sb")
        nc.sync.dma_start(w_sb[:], w_head.rearrange("(p k) v -> p k v", k=KB))

        ones = held.tile([P, P], BF16, name="ones")
        nc.vector.memset(ones[:], 1.0)
        tiny_sq = held.tile([P, N], F32, name="tiny_sq")
        nc.vector.memset(tiny_sq[:], TINY * TINY)
        one = held.tile([P, 1], F32, name="one")
        nc.vector.memset(one[:], 1.0)
        warm_ps = psum.tile([P, S // P, P], F32, name="warm_ps")
        for i in range(WARM_LOADS):
            nc.tensor.matmul(
                warm_ps[:], ones[:], ones[:].unsqueeze(1).to_broadcast([P, S // P, P]), start=True, stop=True
            )
        scratch = held.tile([P, 1], F32, name="scratch")
        nc.scalar.activation(scratch[:], one[:], ACT.Abs_reciprocal_sqrt)
        bias_sb = held.tile([P, MB], F32, name="bias_sb")
        nc.scalar.dma_start(bias_sb[:], b_head.rearrange("(p m) o -> p (m o)", m=MB))
        gain_sq = held.tile([P, KB], F32, name="gain_sq")
        nc.vector.tensor_tensor(gain_sq[:], gain_sb[:], gain_sb[:], MULT)
        gain_cols = [held.tile([P, N], F32, name=f"gain_cols{k}") for k in range(KB)]
        for k in range(KB):
            nc.vector.tensor_scalar(
                gain_cols[k][:], tiny_sq[:], gain_sq[:, k : k + 1], gain_sb[:, k : k + 1], IS_GT, ADD
            )
        inv_gain = held.tile([P, KB], F32, name="inv_gain")
        for k in range(KB):
            nc.vector.reciprocal(inv_gain[:, k : k + 1], gain_cols[k][:, 0:1])

        out_blocks = out.rearrange("(p m) n -> p m n", m=MB)
        w_blocks = w_sb[:].rearrange("p k (q m) -> p k m q", m=MB)
        sums = [psum.tile([P, HN], F32, name=f"sum_ps{h}") for h in range(HALVES)]

        def look_up(k, tokens, halves):
            width = tokens.stop - tokens.start
            gained = held.tile([P, width], F32, name=f"gained{k}_{tokens.start}")
            list_part = offsets[:, tokens.start // 16 : tokens.stop // 16]
            nc.vector.tensor_tensor(
                gained[:], table[k][:].indirect(list_part), gain_cols[k][:, :width], MULT
            )
            hidden = held.tile([P, width], BF16, name=f"hidden{k}_{tokens.start}")
            nc.vector.tensor_scalar(
                hidden[:], gained[:], inv_gain[:, k : k + 1], gain_sb[:, k : k + 1], MULT, MULT
            )
            squares = held.tile([P, width], BF16, name=f"squares{k}_{tokens.start}")
            nc.scalar.activation(squares[:], gained[:], ACT.Square, scale=inv_gain[:, k : k + 1])
            for i, h in enumerate(halves):
                nc.tensor.matmul(
                    sums[h][:], ones[:], squares[:, i * HN : (i + 1) * HN], start=(k == 0), stop=(k == KB - 1)
                )
            return hidden

        rows = [held.tile([P, 2, N], F32, name=f"rows{pair}") for pair in range(0, MB, 2)]
        hidden0 = look_up(0, slice(0, N), range(HALVES))
        for h in range(HALVES):
            tokens = slice(h * HN, (h + 1) * HN)
            hidden = [hidden0[:, tokens], look_up(1, tokens, [h])[:]]
            r = held.tile([P, HN], F32, name=f"r{h}")
            nc.scalar.activation(r[:], sums[h][:], ACT.Abs_reciprocal_sqrt, scale=1.0 / C)

            for pair in range(0, MB, 2):
                logits = psum.tile([P, 2, HN], F32, name=f"logits{h}_{pair}")
                for i in range(2):
                    m = pair + i
                    for k in range(KB):
                        nc.tensor.matmul(
                            logits[:, i, :], w_blocks[:, k, m, :], hidden[k],
                            start=(k == 0), stop=(k == KB - 1),
                        )
                normed = held.tile([P, 2, HN], F32, name=f"normed{h}_{pair}")
                nc.vector.tensor_tensor(
                    normed[:], logits[:], r[:].unsqueeze(1).to_broadcast([P, 2, HN]), MULT
                )
                for i in range(2):
                    bias = bias_sb[:, pair + i : pair + i + 1]
                    if h == HALVES - 1 and i == 1:
                        nc.vector.tensor_scalar_add(rows[pair // 2][:, i, tokens], normed[:, i, :], bias)
                    else:
                        nc.scalar.activation(rows[pair // 2][:, i, tokens], normed[:, i, :], ACT.Identity, bias=bias)
                if h == HALVES - 1:
                    store_queue = nc.scalar if pair == 0 else nc.sync
                    store_queue.dma_start(out_blocks[:, pair : pair + 2, :], rows[pair // 2][:])
